import numpy as np
import ml_dtypes


def mxq(x, axis, fmt="e4m3"):
    dtype, down = {"e4m3": (ml_dtypes.float8_e4m3fn, 7), "e5m2": (ml_dtypes.float8_e5m2, 14)}[fmt]
    v = np.moveaxis(np.asarray(x, np.float32).astype(ml_dtypes.bfloat16).astype(np.float64), axis, -1)
    blocks = v.reshape(v.shape[:-1] + (-1, 32))
    amax = np.abs(blocks).max(-1, keepdims=True)
    byte = np.maximum(np.where(amax > 0, np.frexp(amax)[1] - 1 + 127, 0) - down, 1)
    scale = np.exp2(byte - 127.0)
    codes = (blocks / scale).astype(np.float32).astype(dtype).astype(np.float64)
    return np.moveaxis((codes * scale).reshape(v.shape), -1, axis)


WIDE = False


def mx_kscale(k):
    if not WIDE:
        return np.ones(k)
    levels = np.array([10, -10, 5, -5, 0])
    if k % 512:
        return np.exp2(np.random.permutation(np.resize(levels, k // 32))).repeat(32)
    a = np.empty((k // 512, 16))
    for p in range(k // 512):
        a[p, :8] = np.random.permutation(np.resize(levels, 8))
        for g in range(8):
            far = levels[np.abs(levels - a[p, g]) >= 10]
            a[p, g + 8] = far[np.random.randint(len(far))]
    return np.exp2(a.ravel()).repeat(32)


BF16 = ml_dtypes.bfloat16


def bf(x):
    return np.asarray(x, np.float32).astype(BF16)


def f64(x):
    return np.asarray(x).astype(np.float64)


B, S, HIDDEN, NUM_HEADS, HEAD_DIM = 2, 512, 1024, 16, 64
F = NUM_HEADS * HEAD_DIM


def _split_heads(x):
    b, s, _ = x.shape
    return x.reshape(b, s, NUM_HEADS, HEAD_DIM).transpose(0, 2, 1, 3)


def setup_inputs():
    s = mx_kscale(HIDDEN)
    scale = 1.0 / np.sqrt(HIDDEN)
    return {
        "hidden_states": bf(np.random.standard_normal((B, S, HIDDEN)) * s),
        "Wq": bf(np.random.standard_normal((HIDDEN, F)) * scale / s[:, None]),
        "bq": bf(np.random.standard_normal(F) * 0.5),
        "Wk": bf(np.random.standard_normal((HIDDEN, F)) * scale / s[:, None]),
        "bk": bf(np.random.standard_normal(F) * 0.5),
        "Wv": bf(np.random.standard_normal((HIDDEN, F)) * scale / s[:, None]),
        "bv": bf(np.random.standard_normal(F) * 0.5),
    }


def reference(hidden_states, Wq, bq, Wk, bk, Wv, bv):
    Wqkv = np.concatenate([f64(Wq), f64(Wk), f64(Wv)], axis=1)
    bqkv = np.concatenate([f64(bq), f64(bk), f64(bv)], axis=0)
    qkv = (mxq(f64(hidden_states), 2, "e4m3") @ mxq(Wqkv, 0, "e4m3")) + bqkv
    q, k, v = np.split(qkv, 3, axis=-1)
    return (_split_heads(q), _split_heads(k), _split_heads(v))

@@ -1,0 +1,294 @@
+from contextlib import ExitStack
+
+import concourse.mybir as mybir
+from concourse.masks import make_identity
+
+F32 = mybir.dt.float32
+BF16 = mybir.dt.bfloat16
+U32 = mybir.dt.uint32
+U8 = mybir.dt.uint8
+I32 = mybir.dt.int32
+FP8X4 = mybir.dt.float8_e4m3fn_x4
+ADD = mybir.AluOpType.add
+
+P = 128
+BATCH = 2
+SEQ = 512
+HIDDEN = 1024
+HEADS = 16
+HEAD_DIM = 64
+FEATURES = HEADS * HEAD_DIM
+PASSES = HIDDEN // 512
+TOK = 8
+PAIRS = TOK // 2
+N_BLK = 512
+BLOCKS = 3 * FEATURES // N_BLK
+N_HALF = 256
+HALF_HEADS = N_HALF // HEAD_DIM
+HALVES = 3 * FEATURES // N_HALF
+Q_AFTER = 4
+
+FLOPS = 2 * BATCH * SEQ * HIDDEN * 3 * FEATURES
+
+
+def tile_attention_before_kernel(
+    tc, hidden_states, Wq, bq, Wk, bk, Wv, bv, out_0, out_1, out_2
+):
+    nc = tc.nc
+    weights = (Wq, Wk, Wv)
+    biases = (bq, bk, bv)
+    outs = (out_0, out_1, out_2)
+
+    with ExitStack() as ctx:
+        keep = ctx.enter_context(tc.tile_pool(name="keep", bufs=1))
+        stage = ctx.enter_context(tc.tile_pool(name="stage", bufs=3))
+        result = ctx.enter_context(tc.tile_pool(name="result", bufs=6))
+        psum = ctx.enter_context(tc.psum_pool(name="psum", bufs=8))
+        ctx.enter_context(tc.manual_schedule())
+
+        ident = keep.tile([P, P], F32, name="ident")
+        ones = keep.tile([P, P], BF16, name="ones")
+        braw = keep.tile([1, 3 * FEATURES], BF16, name="braw")
+        brow = keep.tile([P, 3 * FEATURES], BF16, name="brow")
+        bias_sb = keep.tile([P, 3 * FEATURES], BF16, name="bias_sb")
+        x_sb = [keep.tile([P, 2, HIDDEN], BF16, name="x_sb%d" % q) for q in range(PAIRS)]
+        xg = [
+            keep.tile([P, 2, PASSES, P, 4], BF16, name="xg%d" % q, align_bytes=64)
+            for q in range(PAIRS)
+        ]
+        xc = [
+            keep.tile([P, 2, PASSES, P], U32, name="xc%d" % q, align_bytes=64)
+            for q in range(PAIRS)
+        ]
+        xs = [
+            keep.tile([P, 2, PASSES, P], U8, name="xs%d" % q, align_bytes=64)
+            for q in range(PAIRS)
+        ]
+        wr = [
+            [keep.tile([P, 4, FEATURES], BF16, name="wr%d%d" % (t, g)) for g in range(PASSES)]
+            for t in range(3)
+        ]
+        wc = [
+            keep.tile([P, PASSES, N_BLK], U32, name="wc%d" % n, align_bytes=64)
+            for n in range(BLOCKS)
+        ]
+        ws = [
+            keep.tile([P, PASSES, N_BLK], U8, name="ws%d" % n, align_bytes=64)
+            for n in range(BLOCKS)
+        ]
+
+        for t in range(3):
+            nc.scalar.dma_start(
+                out=braw[0:1, t * FEATURES : (t + 1) * FEATURES],
+                in_=biases[t].rearrange("(o n) -> o n", o=1),
+            )
+
+        def load_tokens(q):
+            for b in range(BATCH):
+                nc.sync.dma_start(
+                    out=x_sb[q][b:P:2, :, :],
+                    in_=hidden_states[b].rearrange("(p j) k -> p j k", j=TOK)[
+                        :, 2 * q : 2 * q + 2, :
+                    ],
+                )
+
+        def load_weights(t):
+            for g in range(PASSES):
+                nc.sync.dma_start(
+                    out=wr[t][g][:],
+                    in_=weights[t][512 * g : 512 * (g + 1), :].rearrange(
+                        "(p j) n -> p j n", j=4
+                    ),
+                )
+
+        load_tokens(0)
+        load_weights(0)
+        for q in range(1, PAIRS):
+            load_tokens(q)
+        load_weights(1)
+        load_weights(2)
+
+        nc.vector.memset(brow[:].bitcast(I32), 0)
+        nc.vector.memset(ones[:], 1.0)
+        make_identity(nc, ident[:])
+        nc.vector.tensor_copy(out=brow[0:1, :], in_=braw[0:1, :])
+
+        banks = {}
+
+        def transpose_tokens(j):
+            banks[j] = psum.tile([P, PASSES, 2, P], F32, name="xt", tag="bank")
+            for g in range(PASSES):
+                for u in range(2):
+                    nc.tensor.transpose(
+                        banks[j][:, g, u, :],
+                        x_sb[j // 2][:].bitcast(F32)[:, j % 2, 256 * g + u : 256 * (g + 1) : 2],
+                        ident[:],
+                    )
+
+        def copy_tokens(j, engine):
+            src = banks[j][:].rearrange("p g u t -> p g t u")
+            dst = xg[j // 2][:].bitcast(F32)[:, j % 2]
+            if engine == "v":
+                nc.vector.tensor_copy(out=dst, in_=src)
+            else:
+                nc.scalar.copy(out=dst, in_=src)
+
+        def quantise_tokens(q):
+            nc.vector.quantize_mx(
+                out=xc[q][:].rearrange("p j g c -> p (j g c)").bitcast(FP8X4),
+                scales=xs[q][:].rearrange("p j g c -> p (j g c)"),
+                in_=xg[q][:].rearrange("p j g t w -> p (j g t w)"),
+            )
+
+        def spread_biases():
+            for t in range(3):
+                bp = psum.tile([P, FEATURES], BF16, name="bp", tag="bank")
+                for hf in range(2):
+                    c0 = t * FEATURES + 512 * hf
+                    nc.tensor.matmul(
+                        out=bp[:, 512 * hf : 512 * (hf + 1)],
+                        lhsT=ones[:],
+                        rhs=brow[:, c0 : c0 + 512],
+                        start=True,
+                        stop=True,
+                    )
+                nc.scalar.copy(
+                    out=bias_sb[:, t * FEATURES : (t + 1) * FEATURES], in_=bp[:]
+                )
+
+        grouped = {}
+
+        def regroup(n, g, engine, c0=0, c1=N_BLK):
+            if n not in grouped:
+                grouped[n] = stage.tile(
+                    [P, PASSES, N_BLK, 4], BF16, name="wg", tag="wg", align_bytes=64
+                )
+            t, nb = divmod(n, FEATURES // N_BLK)
+            src = wr[t][g][:, :, nb * N_BLK + c0 : nb * N_BLK + c1].rearrange(
+                "p t (c i) -> p c t i", i=4
+            )
+            dst = grouped[n][:, g, c0:c1, :].rearrange("p (c i) t -> p c t i", i=4)
+            if engine == "v":
+                nc.vector.tensor_copy(out=dst, in_=src)
+            else:
+                nc.scalar.copy(out=dst, in_=src)
+
+        def quantise_pass(n, g):
+            nc.vector.quantize_mx(
+                out=wc[n][:, g, :].bitcast(FP8X4),
+                scales=ws[n][:, g, :],
+                in_=grouped[n][:, g].rearrange("p c t -> p (c t)"),
+            )
+
+        def quantise_block(n):
+            nc.vector.quantize_mx(
+                out=wc[n][:].rearrange("p g c -> p (g c)").bitcast(FP8X4),
+                scales=ws[n][:].rearrange("p g c -> p (g c)"),
+                in_=grouped[n][:].rearrange("p g c t -> p (g c t)"),
+            )
+
+        acc = {}
+
+        def multiply(h, q):
+            acc[(h, q)] = psum.tile([P, 2, N_HALF], F32, name="acc", tag="bank")
+            n, hf = divmod(h, 2)
+            cols = slice(hf * N_HALF, (hf + 1) * N_HALF)
+            for jj in range(2):
+                for g in range(PASSES):
+                    nc.tensor.matmul_mx(
+                        out=acc[(h, q)][:, jj, :],
+                        lhsT=xc[q][:, jj, g, :].bitcast(FP8X4),
+                        lhsT_scale=xs[q][:, jj, g, :],
+                        rhs=wc[n][:, g, cols].bitcast(FP8X4),
+                        rhs_scale=ws[n][:, g, cols],
+                        start=(g == 0),
+                        stop=(g == PASSES - 1),
+                    )
+
+        res = {}
+
+        def evacuate(h, q):
+            if h not in res:
+                res[h] = result.tile(
+                    [P, HALF_HEADS, TOK, HEAD_DIM], F32, name="res", tag="res"
+                )
+            dst = res[h][:, :, 2 * q : 2 * q + 2, :].rearrange("p h j d -> p j h d")
+            sums = acc[(h, q)][:].rearrange("p j (h d) -> p j h d", d=HEAD_DIM)
+            bias = (
+                bias_sb[:, h * N_HALF : (h + 1) * N_HALF]
+                .rearrange("p (h d) -> p h d", d=HEAD_DIM)
+                .unsqueeze(1)
+                .to_broadcast([P, 2, HALF_HEADS, HEAD_DIM])
+            )
+            if q == 0 and (h >= 8 or (h >= 4 and h % 2 == 0)):
+                nc.scalar.copy(out=dst, in_=sums)
+                nc.gpsimd.tensor_tensor(out=dst, in0=dst, in1=bias, op=ADD)
+            else:
+                nc.vector.tensor_tensor(out=dst, in0=sums, in1=bias, op=ADD)
+
+        def store(h):
+            t, hh = divmod(h, FEATURES // N_HALF)
+            for b in range(BATCH):
+                nc.sync.dma_start(
+                    out=outs[t][
+                        b, hh * HALF_HEADS : (hh + 1) * HALF_HEADS
+                    ].rearrange("h (p j) d -> p h (j d)", j=TOK),
+                    in_=res[h][b:P:2].rearrange("p h j d -> p h (j d)"),
+                )
+
+        transpose_tokens(0)
+        transpose_tokens(1)
+        copy_tokens(0, "v")
+        copy_tokens(1, "s")
+        quantise_tokens(0)
+        spread_biases()
+        regroup(0, 0, "v")
+        regroup(1, 0, "s")
+        quantise_pass(0, 0)
+        regroup(0, 1, "v")
+        quantise_pass(0, 1)
+        for q in range(1, PAIRS):
+            transpose_tokens(2 * q)
+            transpose_tokens(2 * q + 1)
+            if q >= 2:
+                evacuate(0, q - 2)
+                evacuate(1, q - 2)
+            copy_tokens(2 * q, "v")
+            copy_tokens(2 * q + 1, "s")
+            quantise_tokens(q)
+            multiply(0, q - 1)
+            multiply(1, q - 1)
+            if q < PAIRS - 1:
+                regroup(1, 1, "s", (q - 1) * N_HALF, q * N_HALF)
+        multiply(0, PAIRS - 1)
+        multiply(1, PAIRS - 1)
+        evacuate(0, 2)
+        evacuate(1, 2)
+        quantise_block(1)
+        for q in range(3):
+            multiply(2, q)
+        evacuate(0, 3)
+        store(0)
+        multiply(2, 3)
+        evacuate(1, 3)
+        store(1)
+        for q in range(PAIRS):
+            multiply(3, q)
+        for g in range(PASSES):
+            regroup(2, g, "s")
+
+        for n in range(1, BLOCKS):
+            more = n + 1 < BLOCKS
+            for k in range(2 * PAIRS):
+                h, q = 2 * n + k // PAIRS, k % PAIRS
+                if n + 2 < BLOCKS and q == 0:
+                    regroup(n + 2, k // PAIRS, "s")
+                if more and k == Q_AFTER:
+                    quantise_block(n + 1)
+                    for kk in range(k):
+                        multiply(2 * n + 2 + kk // PAIRS, kk % PAIRS)
+                evacuate(h, q)
+                if more and k >= Q_AFTER:
+                    multiply(h + 2, q)
+                if q == PAIRS - 1:
+                    store(h)

@@ -18,15 +18,15 @@ HIDDEN = 1024
 HEADS = 16
 HEAD_DIM = 64
 FEATURES = HEADS * HEAD_DIM
-PASSES = HIDDEN // 512
+K_PASS = 512
+PASSES = HIDDEN // K_PASS
 TOK = 8
 PAIRS = TOK // 2
-N_BLK = 512
-BLOCKS = 3 * FEATURES // N_BLK
-N_HALF = 256
-HALF_HEADS = N_HALF // HEAD_DIM
-HALVES = 3 * FEATURES // N_HALF
-Q_AFTER = 4
+GROUP = 256
+GROUP_HEADS = GROUP // HEAD_DIM
+PER_WEIGHT = FEATURES // GROUP
+GROUPS = 3 * PER_WEIGHT
+AHEAD = 6
 
 FLOPS = 2 * BATCH * SEQ * HIDDEN * 3 * FEATURES
 
@@ -41,14 +41,13 @@ def tile_attention_before_kernel(
 
     with ExitStack() as ctx:
         keep = ctx.enter_context(tc.tile_pool(name="keep", bufs=1))
-        stage = ctx.enter_context(tc.tile_pool(name="stage", bufs=3))
-        result = ctx.enter_context(tc.tile_pool(name="result", bufs=6))
+        stage = ctx.enter_context(tc.tile_pool(name="stage", bufs=7))
+        result = ctx.enter_context(tc.tile_pool(name="result", bufs=7))
         psum = ctx.enter_context(tc.psum_pool(name="psum", bufs=8))
         ctx.enter_context(tc.manual_schedule())
 
         ident = keep.tile([P, P], F32, name="ident")
         ones = keep.tile([P, P], BF16, name="ones")
-        braw = keep.tile([1, 3 * FEATURES], BF16, name="braw")
         brow = keep.tile([P, 3 * FEATURES], BF16, name="brow")
         bias_sb = keep.tile([P, 3 * FEATURES], BF16, name="bias_sb")
         x_sb = [keep.tile([P, 2, HIDDEN], BF16, name="x_sb%d" % q) for q in range(PAIRS)]
@@ -69,19 +68,13 @@ def tile_attention_before_kernel(
             for t in range(3)
         ]
         wc = [
-            keep.tile([P, PASSES, N_BLK], U32, name="wc%d" % n, align_bytes=64)
-            for n in range(BLOCKS)
+            keep.tile([P, PASSES, GROUP], U32, name="wc%d" % h, align_bytes=64)
+            for h in range(GROUPS)
         ]
         ws = [
-            keep.tile([P, PASSES, N_BLK], U8, name="ws%d" % n, align_bytes=64)
-            for n in range(BLOCKS)
+            keep.tile([P, PASSES, GROUP], U8, name="ws%d" % h, align_bytes=64)
+            for h in range(GROUPS)
         ]
-
-        for t in range(3):
-            nc.scalar.dma_start(
-                out=braw[0:1, t * FEATURES : (t + 1) * FEATURES],
-                in_=biases[t].rearrange("(o n) -> o n", o=1),
-            )
 
         def load_tokens(q):
             for b in range(BATCH):
@@ -92,46 +85,58 @@ def tile_attention_before_kernel(
                     ],
                 )
 
-        def load_weights(t):
-            for g in range(PASSES):
-                nc.sync.dma_start(
-                    out=wr[t][g][:],
-                    in_=weights[t][512 * g : 512 * (g + 1), :].rearrange(
-                        "(p j) n -> p j n", j=4
-                    ),
-                )
-
-        load_tokens(0)
-        load_weights(0)
-        for q in range(1, PAIRS):
-            load_tokens(q)
-        load_weights(1)
-        load_weights(2)
+        def load_weights(t, g):
+            nc.sync.dma_start(
+                out=wr[t][g][:],
+                in_=weights[t][K_PASS * g : K_PASS * (g + 1), :].rearrange(
+                    "(p j) n -> p j n", j=4
+                ),
+            )
 
         nc.vector.memset(brow[:].bitcast(I32), 0)
         nc.vector.memset(ones[:], 1.0)
         make_identity(nc, ident[:])
-        nc.vector.tensor_copy(out=brow[0:1, :], in_=braw[0:1, :])
+        load_tokens(0)
+        load_weights(0, 0)
+        for t in range(3):
+            nc.sync.dma_start(
+                out=brow[0:1, t * FEATURES : (t + 1) * FEATURES],
+                in_=biases[t].rearrange("(o n) -> o n", o=1),
+            )
+        load_weights(0, 1)
+        for q in range(1, PAIRS):
+            load_tokens(q)
+        for t in range(1, 3):
+            for g in range(PASSES):
+                load_weights(t, g)
+
+        def copy(engine, out, in_):
+            if engine == "v":
+                nc.vector.tensor_copy(out=out, in_=in_)
+            else:
+                nc.scalar.copy(out=out, in_=in_)
 
         banks = {}
 
-        def transpose_tokens(j):
-            banks[j] = psum.tile([P, PASSES, 2, P], F32, name="xt", tag="bank")
-            for g in range(PASSES):
-                for u in range(2):
-                    nc.tensor.transpose(
-                        banks[j][:, g, u, :],
-                        x_sb[j // 2][:].bitcast(F32)[:, j % 2, 256 * g + u : 256 * (g + 1) : 2],
-                        ident[:],
-                    )
+        def transpose_tokens(q):
+            for jj in range(2):
+                j = 2 * q + jj
+                banks[j] = psum.tile([P, PASSES, 2, P], F32, name="xt", tag="bank")
+                words = x_sb[q][:].bitcast(F32)
+                for g in range(PASSES):
+                    for u in range(2):
+                        nc.tensor.transpose(
+                            banks[j][:, g, u, :],
+                            words[:, jj, 256 * g + u : 256 * (g + 1) : 2],
+                            ident[:],
+                        )
 
         def copy_tokens(j, engine):
-            src = banks[j][:].rearrange("p g u t -> p g t u")
-            dst = xg[j // 2][:].bitcast(F32)[:, j % 2]
-            if engine == "v":
-                nc.vector.tensor_copy(out=dst, in_=src)
-            else:
-                nc.scalar.copy(out=dst, in_=src)
+            copy(
+                engine,
+                xg[j // 2][:].bitcast(F32)[:, j % 2],
+                banks[j][:].rearrange("p g u t -> p g t u"),
+            )
 
         def quantise_tokens(q):
             nc.vector.quantize_mx(
@@ -140,67 +145,67 @@ def tile_attention_before_kernel(
                 in_=xg[q][:].rearrange("p j g t w -> p (j g t w)"),
             )
 
-        def spread_biases():
-            for t in range(3):
-                bp = psum.tile([P, FEATURES], BF16, name="bp", tag="bank")
-                for hf in range(2):
-                    c0 = t * FEATURES + 512 * hf
-                    nc.tensor.matmul(
-                        out=bp[:, 512 * hf : 512 * (hf + 1)],
-                        lhsT=ones[:],
-                        rhs=brow[:, c0 : c0 + 512],
-                        start=True,
-                        stop=True,
-                    )
-                nc.scalar.copy(
-                    out=bias_sb[:, t * FEATURES : (t + 1) * FEATURES], in_=bp[:]
+        spread = {}
+
+        def spread_bias(t):
+            spread[t] = psum.tile([P, FEATURES], BF16, name="bp", tag="bank")
+            for hf in range(2):
+                c0 = t * FEATURES + 512 * hf
+                nc.tensor.matmul(
+                    out=spread[t][:, 512 * hf : 512 * (hf + 1)],
+                    lhsT=ones[:],
+                    rhs=brow[:, c0 : c0 + 512],
+                    start=True,
+                    stop=True,
                 )
+
+        def copy_bias(t):
+            nc.scalar.copy(
+                out=bias_sb[:, t * FEATURES : (t + 1) * FEATURES], in_=spread[t][:]
+            )
 
         grouped = {}
 
-        def regroup(n, g, engine, c0=0, c1=N_BLK):
-            if n not in grouped:
-                grouped[n] = stage.tile(
-                    [P, PASSES, N_BLK, 4], BF16, name="wg", tag="wg", align_bytes=64
+        def regroup(h, g, engine):
+            if h not in grouped:
+                grouped[h] = stage.tile(
+                    [P, PASSES, GROUP, 4], BF16, name="wg", tag="wg", align_bytes=64
                 )
-            t, nb = divmod(n, FEATURES // N_BLK)
-            src = wr[t][g][:, :, nb * N_BLK + c0 : nb * N_BLK + c1].rearrange(
-                "p t (c i) -> p c t i", i=4
-            )
-            dst = grouped[n][:, g, c0:c1, :].rearrange("p (c i) t -> p c t i", i=4)
-            if engine == "v":
-                nc.vector.tensor_copy(out=dst, in_=src)
-            else:
-                nc.scalar.copy(out=dst, in_=src)
-
-        def quantise_pass(n, g):
-            nc.vector.quantize_mx(
-                out=wc[n][:, g, :].bitcast(FP8X4),
-                scales=ws[n][:, g, :],
-                in_=grouped[n][:, g].rearrange("p c t -> p (c t)"),
+            t, hh = divmod(h, PER_WEIGHT)
+            copy(
+                engine,
+                grouped[h][:, g].rearrange("p (c i) t -> p c t i", i=4),
+                wr[t][g][:, :, hh * GROUP : (hh + 1) * GROUP].rearrange(
+                    "p t (c i) -> p c t i", i=4
+                ),
             )
 
-        def quantise_block(n):
+        def quantise_pass(h, g):
             nc.vector.quantize_mx(
-                out=wc[n][:].rearrange("p g c -> p (g c)").bitcast(FP8X4),
-                scales=ws[n][:].rearrange("p g c -> p (g c)"),
-                in_=grouped[n][:].rearrange("p g c t -> p (g c t)"),
+                out=wc[h][:, g, :].bitcast(FP8X4),
+                scales=ws[h][:, g, :],
+                in_=grouped[h][:, g].rearrange("p c t -> p (c t)"),
+            )
+
+        def quantise_group(h):
+            nc.vector.quantize_mx(
+                out=wc[h][:].rearrange("p g c -> p (g c)").bitcast(FP8X4),
+                scales=ws[h][:].rearrange("p g c -> p (g c)"),
+                in_=grouped[h][:].rearrange("p g c t -> p (g c t)"),
             )
 
         acc = {}
 
         def multiply(h, q):
-            acc[(h, q)] = psum.tile([P, 2, N_HALF], F32, name="acc", tag="bank")
-            n, hf = divmod(h, 2)
-            cols = slice(hf * N_HALF, (hf + 1) * N_HALF)
+            acc[(h, q)] = psum.tile([P, 2, GROUP], F32, name="acc", tag="bank")
             for jj in range(2):
                 for g in range(PASSES):
                     nc.tensor.matmul_mx(
                         out=acc[(h, q)][:, jj, :],
                         lhsT=xc[q][:, jj, g, :].bitcast(FP8X4),
                         lhsT_scale=xs[q][:, jj, g, :],
-                        rhs=wc[n][:, g, cols].bitcast(FP8X4),
-                        rhs_scale=ws[n][:, g, cols],
+                        rhs=wc[h][:, g, :].bitcast(FP8X4),
+                        rhs_scale=ws[h][:, g, :],
                         start=(g == 0),
                         stop=(g == PASSES - 1),
                     )
@@ -210,85 +215,106 @@ def tile_attention_before_kernel(
         def evacuate(h, q):
             if h not in res:
                 res[h] = result.tile(
-                    [P, HALF_HEADS, TOK, HEAD_DIM], F32, name="res", tag="res"
+                    [P, GROUP_HEADS, TOK, HEAD_DIM], F32, name="res", tag="res"
                 )
             dst = res[h][:, :, 2 * q : 2 * q + 2, :].rearrange("p h j d -> p j h d")
             sums = acc[(h, q)][:].rearrange("p j (h d) -> p j h d", d=HEAD_DIM)
             bias = (
-                bias_sb[:, h * N_HALF : (h + 1) * N_HALF]
+                bias_sb[:, h * GROUP : (h + 1) * GROUP]
                 .rearrange("p (h d) -> p h d", d=HEAD_DIM)
                 .unsqueeze(1)
-                .to_broadcast([P, 2, HALF_HEADS, HEAD_DIM])
+                .to_broadcast([P, 2, GROUP_HEADS, HEAD_DIM])
             )
-            if q == 0 and (h >= 8 or (h >= 4 and h % 2 == 0)):
+            if q == 0 and 4 <= h < GROUPS - 1:
                 nc.scalar.copy(out=dst, in_=sums)
                 nc.gpsimd.tensor_tensor(out=dst, in0=dst, in1=bias, op=ADD)
             else:
                 nc.vector.tensor_tensor(out=dst, in0=sums, in1=bias, op=ADD)
 
         def store(h):
-            t, hh = divmod(h, FEATURES // N_HALF)
+            t, hh = divmod(h, PER_WEIGHT)
             for b in range(BATCH):
                 nc.sync.dma_start(
                     out=outs[t][
-                        b, hh * HALF_HEADS : (hh + 1) * HALF_HEADS
+                        b, hh * GROUP_HEADS : (hh + 1) * GROUP_HEADS
                     ].rearrange("h (p j) d -> p h (j d)", j=TOK),
                     in_=res[h][b:P:2].rearrange("p h j d -> p h (j d)"),
                 )
 
         transpose_tokens(0)
-        transpose_tokens(1)
         copy_tokens(0, "v")
         copy_tokens(1, "s")
         quantise_tokens(0)
-        spread_biases()
+        spread_bias(0)
         regroup(0, 0, "v")
-        regroup(1, 0, "s")
+        regroup(1, 0, "v")
+        regroup(2, 0, "s")
+        copy_bias(0)
         quantise_pass(0, 0)
+        quantise_pass(1, 0)
         regroup(0, 1, "v")
+        regroup(1, 1, "v")
+        regroup(2, 1, "s")
+        regroup(3, 0, "s")
         quantise_pass(0, 1)
-        for q in range(1, PAIRS):
-            transpose_tokens(2 * q)
-            transpose_tokens(2 * q + 1)
-            if q >= 2:
-                evacuate(0, q - 2)
-                evacuate(1, q - 2)
-            copy_tokens(2 * q, "v")
-            copy_tokens(2 * q + 1, "s")
-            quantise_tokens(q)
-            multiply(0, q - 1)
-            multiply(1, q - 1)
-            if q < PAIRS - 1:
-                regroup(1, 1, "s", (q - 1) * N_HALF, q * N_HALF)
-        multiply(0, PAIRS - 1)
-        multiply(1, PAIRS - 1)
+        quantise_pass(1, 1)
+        transpose_tokens(1)
+        copy_tokens(2, "s")
+        copy_tokens(3, "s")
+        multiply(0, 0)
+        regroup(3, 1, "v")
+        evacuate(0, 0)
+        transpose_tokens(2)
+        copy_tokens(4, "s")
+        copy_tokens(5, "s")
+        quantise_tokens(1)
+        quantise_group(2)
+        transpose_tokens(3)
+        copy_tokens(6, "s")
+        copy_tokens(7, "s")
+        quantise_tokens(2)
+        quantise_group(3)
+        quantise_tokens(3)
+        multiply(0, 1)
+        multiply(0, 2)
+        multiply(0, 3)
+        spread_bias(1)
+        multiply(1, 0)
+        multiply(1, 1)
+        multiply(1, 2)
+        regroup(4, 0, "s")
+        copy_bias(1)
+        regroup(4, 1, "s")
+        evacuate(0, 1)
+        multiply(1, 3)
         evacuate(0, 2)
-        evacuate(1, 2)
-        quantise_block(1)
-        for q in range(3):
-            multiply(2, q)
+        spread_bias(2)
+        regroup(5, 0, "s")
+        copy_bias(2)
+        regroup(5, 1, "s")
         evacuate(0, 3)
         store(0)
-        multiply(2, 3)
-        evacuate(1, 3)
-        store(1)
+        multiply(2, 0)
         for q in range(PAIRS):
-            multiply(3, q)
-        for g in range(PASSES):
-            regroup(2, g, "s")
+            evacuate(1, q)
+            if q < 3:
+                multiply(2, q + 1)
+            else:
+                multiply(3, 0)
+        store(1)
+        multiply(3, 1)
+        regroup(6, 0, "s")
+        regroup(6, 1, "s")
 
-        for n in range(1, BLOCKS):
-            more = n + 1 < BLOCKS
-            for k in range(2 * PAIRS):
-                h, q = 2 * n + k // PAIRS, k % PAIRS
-                if n + 2 < BLOCKS and q == 0:
-                    regroup(n + 2, k // PAIRS, "s")
-                if more and k == Q_AFTER:
-                    quantise_block(n + 1)
-                    for kk in range(k):
-                        multiply(2 * n + 2 + kk // PAIRS, kk % PAIRS)
+        for h in range(2, GROUPS):
+            for q in range(PAIRS):
+                if q == 2 and h + 2 < GROUPS:
+                    quantise_group(h + 2)
                 evacuate(h, q)
-                if more and k >= Q_AFTER:
-                    multiply(h + 2, q)
-                if q == PAIRS - 1:
-                    store(h)
+                if q == 0 and 7 <= h + 4 < GROUPS:
+                    for g in range(PASSES):
+                        regroup(h + 4, g, "s")
+                nxt = h * PAIRS + q + AHEAD
+                if nxt < GROUPS * PAIRS:
+                    multiply(nxt // PAIRS, nxt % PAIRS)
+            store(h)

@@ -225,7 +225,7 @@ def tile_attention_before_kernel(
                 .unsqueeze(1)
                 .to_broadcast([P, 2, GROUP_HEADS, HEAD_DIM])
             )
-            if q == 0 and 4 <= h < GROUPS - 1:
+            if q == 0 and h % 2 == 0 and h >= 4 or q == 1 and h >= 10:
                 nc.scalar.copy(out=dst, in_=sums)
                 nc.gpsimd.tensor_tensor(out=dst, in0=dst, in1=bias, op=ADD)
             else:

@@ -47,6 +47,7 @@ def tile_attention_before_kernel(
         ctx.enter_context(tc.manual_schedule())
 
         ident = keep.tile([P, P], F32, name="ident")
+        perm = keep.tile([P, P], F32, name="perm")
         ones = keep.tile([P, P], BF16, name="ones")
         brow = keep.tile([P, 3 * FEATURES], BF16, name="brow")
         bias_sb = keep.tile([P, 3 * FEATURES], BF16, name="bias_sb")
@@ -77,13 +78,12 @@ def tile_attention_before_kernel(
         ]
 
         def load_tokens(q):
-            for b in range(BATCH):
-                nc.sync.dma_start(
-                    out=x_sb[q][b:P:2, :, :],
-                    in_=hidden_states[b].rearrange("(p j) k -> p j k", j=TOK)[
-                        :, 2 * q : 2 * q + 2, :
-                    ],
-                )
+            nc.sync.dma_start(
+                out=x_sb[q][:],
+                in_=hidden_states.rearrange("b (p j) k -> (b p) j k", j=TOK)[
+                    :, 2 * q : 2 * q + 2, :
+                ],
+            )
 
         def load_weights(t, g):
             nc.sync.dma_start(
@@ -96,6 +96,10 @@ def tile_attention_before_kernel(
         nc.vector.memset(brow[:].bitcast(I32), 0)
         nc.vector.memset(ones[:], 1.0)
         make_identity(nc, ident[:])
+        nc.vector.tensor_copy(
+            out=perm[:].rearrange("k (p b) -> k p b", b=BATCH),
+            in_=ident[:].rearrange("k (b p) -> k p b", b=BATCH),
+        )
         load_tokens(0)
         load_weights(0, 0)
         for t in range(3):
@@ -128,7 +132,7 @@ def tile_attention_before_kernel(
                         nc.tensor.transpose(
                             banks[j][:, g, u, :],
                             words[:, jj, 256 * g + u : 256 * (g + 1) : 2],
-                            ident[:],
+                            perm[:],
                         )
 
         def copy_tokens(j, engine):

@@ -41,8 +41,8 @@ def tile_attention_before_kernel(
 
     with ExitStack() as ctx:
         keep = ctx.enter_context(tc.tile_pool(name="keep", bufs=1))
-        stage = ctx.enter_context(tc.tile_pool(name="stage", bufs=7))
-        result = ctx.enter_context(tc.tile_pool(name="result", bufs=7))
+        stage = ctx.enter_context(tc.tile_pool(name="stage", bufs=5))
+        result = ctx.enter_context(tc.tile_pool(name="result", bufs=9))
         psum = ctx.enter_context(tc.psum_pool(name="psum", bufs=8))
         ctx.enter_context(tc.manual_schedule())
 
@@ -101,6 +101,7 @@ def tile_attention_before_kernel(
             in_=ident[:].rearrange("k (b p) -> k p b", b=BATCH),
         )
         load_tokens(0)
+        load_tokens(1)
         load_weights(0, 0)
         for t in range(3):
             nc.sync.dma_start(
@@ -108,7 +109,7 @@ def tile_attention_before_kernel(
                 in_=biases[t].rearrange("(o n) -> o n", o=1),
             )
         load_weights(0, 1)
-        for q in range(1, PAIRS):
+        for q in range(2, PAIRS):
             load_tokens(q)
         for t in range(1, 3):
             for g in range(PASSES):
@@ -229,7 +230,7 @@ def tile_attention_before_kernel(
                 .unsqueeze(1)
                 .to_broadcast([P, 2, GROUP_HEADS, HEAD_DIM])
             )
-            if q == 0 and h % 2 == 0 and h >= 4 or q == 1 and h >= 10:
+            if q == 0 and h >= 5:
                 nc.scalar.copy(out=dst, in_=sums)
                 nc.gpsimd.tensor_tensor(out=dst, in0=dst, in1=bias, op=ADD)
             else:
@@ -248,64 +249,65 @@ def tile_attention_before_kernel(
         transpose_tokens(0)
         copy_tokens(0, "v")
         copy_tokens(1, "s")
+        transpose_tokens(1)
+        copy_tokens(2, "v")
+        copy_tokens(3, "s")
         quantise_tokens(0)
-        spread_bias(0)
+        for t in range(3):
+            spread_bias(t)
         regroup(0, 0, "v")
+        quantise_tokens(1)
         regroup(1, 0, "v")
         regroup(2, 0, "s")
-        copy_bias(0)
         quantise_pass(0, 0)
-        quantise_pass(1, 0)
+        copy_bias(0)
+        copy_bias(1)
         regroup(0, 1, "v")
+        quantise_pass(1, 0)
+        quantise_pass(0, 1)
         regroup(1, 1, "v")
         regroup(2, 1, "s")
-        regroup(3, 0, "s")
-        quantise_pass(0, 1)
-        quantise_pass(1, 1)
-        transpose_tokens(1)
-        copy_tokens(2, "s")
-        copy_tokens(3, "s")
+        copy_bias(2)
         multiply(0, 0)
-        regroup(3, 1, "v")
-        evacuate(0, 0)
+        multiply(0, 1)
         transpose_tokens(2)
+        quantise_pass(1, 1)
+        evacuate(0, 0)
         copy_tokens(4, "s")
         copy_tokens(5, "s")
-        quantise_tokens(1)
-        quantise_group(2)
         transpose_tokens(3)
+        regroup(3, 0, "v")
+        evacuate(0, 1)
         copy_tokens(6, "s")
         copy_tokens(7, "s")
+        quantise_group(2)
         quantise_tokens(2)
-        quantise_group(3)
-        quantise_tokens(3)
-        multiply(0, 1)
-        multiply(0, 2)
-        multiply(0, 3)
-        spread_bias(1)
+        regroup(3, 1, "v")
         multiply(1, 0)
         multiply(1, 1)
+        multiply(0, 2)
+        evacuate(1, 0)
+        quantise_tokens(3)
+        quantise_group(3)
+        multiply(0, 3)
         multiply(1, 2)
+        evacuate(1, 1)
         regroup(4, 0, "s")
-        copy_bias(1)
         regroup(4, 1, "s")
-        evacuate(0, 1)
         multiply(1, 3)
+        multiply(2, 0)
         evacuate(0, 2)
-        spread_bias(2)
+        multiply(2, 1)
         regroup(5, 0, "s")
-        copy_bias(2)
         regroup(5, 1, "s")
         evacuate(0, 3)
         store(0)
-        multiply(2, 0)
-        for q in range(PAIRS):
-            evacuate(1, q)
-            if q < 3:
-                multiply(2, q + 1)
-            else:
-                multiply(3, 0)
+        multiply(2, 2)
+        evacuate(1, 2)
+        multiply(2, 3)
+        evacuate(1, 3)
         store(1)
+        multiply(3, 0)
         multiply(3, 1)
         regroup(6, 0, "s")
         regroup(6, 1, "s")

from contextlib import ExitStack

import concourse.mybir as mybir
from concourse.masks import make_identity

F32 = mybir.dt.float32
BF16 = mybir.dt.bfloat16
U32 = mybir.dt.uint32
U8 = mybir.dt.uint8
I32 = mybir.dt.int32
FP8X4 = mybir.dt.float8_e4m3fn_x4
ADD = mybir.AluOpType.add

P = 128
BATCH = 2
SEQ = 512
HIDDEN = 1024
HEADS = 16
HEAD_DIM = 64
FEATURES = HEADS * HEAD_DIM
K_PASS = 512
PASSES = HIDDEN // K_PASS
TOK = 8
PAIRS = TOK // 2
GROUP = 256
GROUP_HEADS = GROUP // HEAD_DIM
PER_WEIGHT = FEATURES // GROUP
GROUPS = 3 * PER_WEIGHT
AHEAD = 6

FLOPS = 2 * BATCH * SEQ * HIDDEN * 3 * FEATURES


def tile_attention_before_kernel(
    tc, hidden_states, Wq, bq, Wk, bk, Wv, bv, out_0, out_1, out_2
):
    nc = tc.nc
    weights = (Wq, Wk, Wv)
    biases = (bq, bk, bv)
    outs = (out_0, out_1, out_2)

    with ExitStack() as ctx:
        keep = ctx.enter_context(tc.tile_pool(name="keep", bufs=1))
        stage = ctx.enter_context(tc.tile_pool(name="stage", bufs=5))
        result = ctx.enter_context(tc.tile_pool(name="result", bufs=9))
        psum = ctx.enter_context(tc.psum_pool(name="psum", bufs=8))
        ctx.enter_context(tc.manual_schedule())

        ident = keep.tile([P, P], F32, name="ident")
        perm = keep.tile([P, P], F32, name="perm")
        ones = keep.tile([P, P], BF16, name="ones")
        brow = keep.tile([P, 3 * FEATURES], BF16, name="brow")
        bias_sb = keep.tile([P, 3 * FEATURES], BF16, name="bias_sb")
        x_sb = [keep.tile([P, 2, HIDDEN], BF16, name="x_sb%d" % q) for q in range(PAIRS)]
        xg = [
            keep.tile([P, 2, PASSES, P, 4], BF16, name="xg%d" % q, align_bytes=64)
            for q in range(PAIRS)
        ]
        xc = [
            keep.tile([P, 2, PASSES, P], U32, name="xc%d" % q, align_bytes=64)
            for q in range(PAIRS)
        ]
        xs = [
            keep.tile([P, 2, PASSES, P], U8, name="xs%d" % q, align_bytes=64)
            for q in range(PAIRS)
        ]
        wr = [
            [keep.tile([P, 4, FEATURES], BF16, name="wr%d%d" % (t, g)) for g in range(PASSES)]
            for t in range(3)
        ]
        wc = [
            keep.tile([P, PASSES, GROUP], U32, name="wc%d" % h, align_bytes=64)
            for h in range(GROUPS)
        ]
        ws = [
            keep.tile([P, PASSES, GROUP], U8, name="ws%d" % h, align_bytes=64)
            for h in range(GROUPS)
        ]

        def load_tokens(q):
            nc.sync.dma_start(
                out=x_sb[q][:],
                in_=hidden_states.rearrange("b (p j) k -> (b p) j k", j=TOK)[
                    :, 2 * q : 2 * q + 2, :
                ],
            )

        def load_weights(t, g):
            nc.sync.dma_start(
                out=wr[t][g][:],
                in_=weights[t][K_PASS * g : K_PASS * (g + 1), :].rearrange(
                    "(p j) n -> p j n", j=4
                ),
            )

        nc.vector.memset(brow[:].bitcast(I32), 0)
        nc.vector.memset(ones[:], 1.0)
        make_identity(nc, ident[:])
        nc.vector.tensor_copy(
            out=perm[:].rearrange("k (p b) -> k p b", b=BATCH),
            in_=ident[:].rearrange("k (b p) -> k p b", b=BATCH),
        )
        load_tokens(0)
        load_tokens(1)
        load_weights(0, 0)
        for t in range(3):
            nc.sync.dma_start(
                out=brow[0:1, t * FEATURES : (t + 1) * FEATURES],
                in_=biases[t].rearrange("(o n) -> o n", o=1),
            )
        load_weights(0, 1)
        for q in range(2, PAIRS):
            load_tokens(q)
        for t in range(1, 3):
            for g in range(PASSES):
                load_weights(t, g)

        def copy(engine, out, in_):
            if engine == "v":
                nc.vector.tensor_copy(out=out, in_=in_)
            else:
                nc.scalar.copy(out=out, in_=in_)

        banks = {}

        def transpose_tokens(q):
            for jj in range(2):
                j = 2 * q + jj
                banks[j] = psum.tile([P, PASSES, 2, P], F32, name="xt", tag="bank")
                words = x_sb[q][:].bitcast(F32)
                for g in range(PASSES):
                    for u in range(2):
                        nc.tensor.transpose(
                            banks[j][:, g, u, :],
                            words[:, jj, 256 * g + u : 256 * (g + 1) : 2],
                            perm[:],
                        )

        def copy_tokens(j, engine):
            copy(
                engine,
                xg[j // 2][:].bitcast(F32)[:, j % 2],
                banks[j][:].rearrange("p g u t -> p g t u"),
            )

        def quantise_tokens(q):
            nc.vector.quantize_mx(
                out=xc[q][:].rearrange("p j g c -> p (j g c)").bitcast(FP8X4),
                scales=xs[q][:].rearrange("p j g c -> p (j g c)"),
                in_=xg[q][:].rearrange("p j g t w -> p (j g t w)"),
            )

        spread = {}

        def spread_bias(t):
            spread[t] = psum.tile([P, FEATURES], BF16, name="bp", tag="bank")
            for hf in range(2):
                c0 = t * FEATURES + 512 * hf
                nc.tensor.matmul(
                    out=spread[t][:, 512 * hf : 512 * (hf + 1)],
                    lhsT=ones[:],
                    rhs=brow[:, c0 : c0 + 512],
                    start=True,
                    stop=True,
                )

        def copy_bias(t):
            nc.scalar.copy(
                out=bias_sb[:, t * FEATURES : (t + 1) * FEATURES], in_=spread[t][:]
            )

        grouped = {}

        def regroup(h, g, engine):
            if h not in grouped:
                grouped[h] = stage.tile(
                    [P, PASSES, GROUP, 4], BF16, name="wg", tag="wg", align_bytes=64
                )
            t, hh = divmod(h, PER_WEIGHT)
            copy(
                engine,
                grouped[h][:, g].rearrange("p (c i) t -> p c t i", i=4),
                wr[t][g][:, :, hh * GROUP : (hh + 1) * GROUP].rearrange(
                    "p t (c i) -> p c t i", i=4
                ),
            )

        def quantise_pass(h, g):
            nc.vector.quantize_mx(
                out=wc[h][:, g, :].bitcast(FP8X4),
                scales=ws[h][:, g, :],
                in_=grouped[h][:, g].rearrange("p c t -> p (c t)"),
            )

        def quantise_group(h):
            nc.vector.quantize_mx(
                out=wc[h][:].rearrange("p g c -> p (g c)").bitcast(FP8X4),
                scales=ws[h][:].rearrange("p g c -> p (g c)"),
                in_=grouped[h][:].rearrange("p g c t -> p (g c t)"),
            )

        acc = {}

        def multiply(h, q):
            acc[(h, q)] = psum.tile([P, 2, GROUP], F32, name="acc", tag="bank")
            for jj in range(2):
                for g in range(PASSES):
                    nc.tensor.matmul_mx(
                        out=acc[(h, q)][:, jj, :],
                        lhsT=xc[q][:, jj, g, :].bitcast(FP8X4),
                        lhsT_scale=xs[q][:, jj, g, :],
                        rhs=wc[h][:, g, :].bitcast(FP8X4),
                        rhs_scale=ws[h][:, g, :],
                        start=(g == 0),
                        stop=(g == PASSES - 1),
                    )

        res = {}

        def evacuate(h, q):
            if h not in res:
                res[h] = result.tile(
                    [P, GROUP_HEADS, TOK, HEAD_DIM], F32, name="res", tag="res"
                )
            dst = res[h][:, :, 2 * q : 2 * q + 2, :].rearrange("p h j d -> p j h d")
            sums = acc[(h, q)][:].rearrange("p j (h d) -> p j h d", d=HEAD_DIM)
            bias = (
                bias_sb[:, h * GROUP : (h + 1) * GROUP]
                .rearrange("p (h d) -> p h d", d=HEAD_DIM)
                .unsqueeze(1)
                .to_broadcast([P, 2, GROUP_HEADS, HEAD_DIM])
            )
            if q == 0 and h >= 5:
                nc.scalar.copy(out=dst, in_=sums)
                nc.gpsimd.tensor_tensor(out=dst, in0=dst, in1=bias, op=ADD)
            else:
                nc.vector.tensor_tensor(out=dst, in0=sums, in1=bias, op=ADD)

        def store(h):
            t, hh = divmod(h, PER_WEIGHT)
            for b in range(BATCH):
                nc.sync.dma_start(
                    out=outs[t][
                        b, hh * GROUP_HEADS : (hh + 1) * GROUP_HEADS
                    ].rearrange("h (p j) d -> p h (j d)", j=TOK),
                    in_=res[h][b:P:2].rearrange("p h j d -> p h (j d)"),
                )

        transpose_tokens(0)
        copy_tokens(0, "v")
        copy_tokens(1, "s")
        transpose_tokens(1)
        copy_tokens(2, "v")
        copy_tokens(3, "s")
        quantise_tokens(0)
        for t in range(3):
            spread_bias(t)
        regroup(0, 0, "v")
        quantise_tokens(1)
        regroup(1, 0, "v")
        regroup(2, 0, "s")
        quantise_pass(0, 0)
        copy_bias(0)
        copy_bias(1)
        regroup(0, 1, "v")
        quantise_pass(1, 0)
        quantise_pass(0, 1)
        regroup(1, 1, "v")
        regroup(2, 1, "s")
        copy_bias(2)
        multiply(0, 0)
        multiply(0, 1)
        transpose_tokens(2)
        quantise_pass(1, 1)
        evacuate(0, 0)
        copy_tokens(4, "s")
        copy_tokens(5, "s")
        transpose_tokens(3)
        regroup(3, 0, "v")
        evacuate(0, 1)
        copy_tokens(6, "s")
        copy_tokens(7, "s")
        quantise_group(2)
        quantise_tokens(2)
        regroup(3, 1, "v")
        multiply(1, 0)
        multiply(1, 1)
        multiply(0, 2)
        evacuate(1, 0)
        quantise_tokens(3)
        quantise_group(3)
        multiply(0, 3)
        multiply(1, 2)
        evacuate(1, 1)
        regroup(4, 0, "s")
        regroup(4, 1, "s")
        multiply(1, 3)
        multiply(2, 0)
        evacuate(0, 2)
        multiply(2, 1)
        regroup(5, 0, "s")
        regroup(5, 1, "s")
        evacuate(0, 3)
        store(0)
        multiply(2, 2)
        evacuate(1, 2)
        multiply(2, 3)
        evacuate(1, 3)
        store(1)
        multiply(3, 0)
        multiply(3, 1)
        regroup(6, 0, "s")
        regroup(6, 1, "s")

        for h in range(2, GROUPS):
            for q in range(PAIRS):
                if q == 2 and h + 2 < GROUPS:
                    quantise_group(h + 2)
                evacuate(h, q)
                if q == 0 and 7 <= h + 4 < GROUPS:
                    for g in range(PASSES):
                        regroup(h + 4, g, "s")
                nxt = h * PAIRS + q + AHEAD
                if nxt < GROUPS * PAIRS:
                    multiply(nxt // PAIRS, nxt % PAIRS)
            store(h)
